import numpy as np
import ml_dtypes

BF16 = ml_dtypes.bfloat16


def bf(x):
    return np.asarray(x, np.float32).astype(BF16)


def f32(x):
    return np.asarray(x, np.float32)


def f64(x):
    return np.asarray(x).astype(np.float64)


def striped(idx):
    return np.tile(idx.reshape(-1, 16).T, (8, 1))


K, R, L, S, N = 128, 128, 128, 1024, 256


def setup_inputs():
    return {"table": bf(np.random.standard_normal((K, S))), "k1": bf(np.random.standard_normal((K, R)) / np.sqrt(K)), "b1": f32(0.1 * np.random.standard_normal((R, 1))), "k2": bf(np.random.standard_normal((R, R)) / np.sqrt(R)), "b2": f32(0.1 * np.random.standard_normal((R, 1))), "k3": bf(np.random.standard_normal((R, L)) / np.sqrt(R)), "b3": f32(0.1 * np.random.standard_normal((L, 1))), "offs": striped(np.random.permutation(S)[:N])}


def reference(table, k1, b1, k2, b2, k3, b3, offs):
    idx = offs[:16].T.reshape(-1)
    h1 = f64(k1).T @ f64(table)[:, idx] + f64(b1)
    h2 = f64(k2).T @ h1 + f64(b2)
    return f64(k3).T @ h2 + f64(b3)

@@ -1,0 +1,49 @@
+import concourse.mybir as mybir
+
+P = 128
+S = 1024
+N = 256
+
+FLOPS = 3 * 2 * P * P * N
+
+BF16 = mybir.dt.bfloat16
+F32 = mybir.dt.float32
+U16 = mybir.dt.uint16
+ADD = mybir.AluOpType.add
+
+
+def tile_switchnet_fstar_kernel(tc, table, k1, b1, k2, b2, k3, b3, offs, out):
+    nc = tc.nc
+    with (
+        tc.tile_pool(name="held", bufs=1) as held,
+        tc.psum_pool(name="psum", bufs=1) as psum,
+    ):
+        offsets = held.tile([P, N // 16], U16, name="offsets")
+        nc.sync.dma_start(offsets[:], offs)
+        samples = held.tile([P, S], BF16, name="samples")
+        nc.sync.dma_start(samples[:], table)
+        weights = []
+        biases = []
+        for stage, (k, b) in enumerate(((k1, b1), (k2, b2), (k3, b3))):
+            weight = held.tile([P, P], BF16, name=f"weight{stage}")
+            nc.sync.dma_start(weight[:], k)
+            bias = held.tile([P, 1], F32, name=f"bias{stage}")
+            nc.sync.dma_start(bias[:], b)
+            weights.append(weight)
+            biases.append(bias)
+
+        sum1 = psum.tile([P, N], F32, name="sum1")
+        nc.tensor.matmul(sum1[:], weights[0][:], samples[:].indirect(offsets[:]))
+        h1 = held.tile([P, N], BF16, name="h1")
+        nc.vector.tensor_scalar(h1[:], sum1[:], biases[0][:], None, ADD)
+
+        sum2 = psum.tile([P, N], F32, name="sum2")
+        nc.tensor.matmul(sum2[:], weights[1][:], h1[:])
+        h2 = held.tile([P, N], BF16, name="h2")
+        nc.vector.tensor_scalar(h2[:], sum2[:], biases[1][:], None, ADD)
+
+        sum3 = psum.tile([P, N], F32, name="sum3")
+        nc.tensor.matmul(sum3[:], weights[2][:], h2[:])
+        result = held.tile([P, N], F32, name="result")
+        nc.vector.tensor_scalar(result[:], sum3[:], biases[2][:], None, ADD)
+        nc.sync.dma_start(out, result[:])

@@ -24,11 +24,13 @@ def tile_switchnet_fstar_kernel(tc, table, k1, b1, k2, b2, k3, b3, offs, out):
         nc.sync.dma_start(samples[:], table)
         weights = []
         biases = []
-        for stage, (k, b) in enumerate(((k1, b1), (k2, b2), (k3, b3))):
+        for stage, (k, b, queue) in enumerate(
+            ((k1, b1, nc.scalar), (k2, b2, nc.scalar), (k3, b3, nc.gpsimd))
+        ):
             weight = held.tile([P, P], BF16, name=f"weight{stage}")
-            nc.sync.dma_start(weight[:], k)
+            queue.dma_start(weight[:], k)
             bias = held.tile([P, 1], F32, name=f"bias{stage}")
-            nc.sync.dma_start(bias[:], b)
+            queue.dma_start(bias[:], b)
             weights.append(weight)
             biases.append(bias)
 

@@ -3,6 +3,7 @@ import concourse.mybir as mybir
 P = 128
 S = 1024
 N = 256
+HALF = N // 2
 
 FLOPS = 3 * 2 * P * P * N
 
@@ -10,6 +11,7 @@ BF16 = mybir.dt.bfloat16
 F32 = mybir.dt.float32
 U16 = mybir.dt.uint16
 ADD = mybir.AluOpType.add
+IDENTITY = mybir.ActivationFunctionType.Identity
 
 
 def tile_switchnet_fstar_kernel(tc, table, k1, b1, k2, b2, k3, b3, offs, out):
@@ -34,18 +36,24 @@ def tile_switchnet_fstar_kernel(tc, table, k1, b1, k2, b2, k3, b3, offs, out):
             weights.append(weight)
             biases.append(bias)
 
-        sum1 = psum.tile([P, N], F32, name="sum1")
-        nc.tensor.matmul(sum1[:], weights[0][:], samples[:].indirect(offsets[:]))
-        h1 = held.tile([P, N], BF16, name="h1")
-        nc.vector.tensor_scalar(h1[:], sum1[:], biases[0][:], None, ADD)
-
-        sum2 = psum.tile([P, N], F32, name="sum2")
-        nc.tensor.matmul(sum2[:], weights[1][:], h1[:])
-        h2 = held.tile([P, N], BF16, name="h2")
-        nc.vector.tensor_scalar(h2[:], sum2[:], biases[1][:], None, ADD)
-
-        sum3 = psum.tile([P, N], F32, name="sum3")
-        nc.tensor.matmul(sum3[:], weights[2][:], h2[:])
         result = held.tile([P, N], F32, name="result")
-        nc.vector.tensor_scalar(result[:], sum3[:], biases[2][:], None, ADD)
+
+        moving = [
+            samples[:].indirect(offsets[:, half * (HALF // 16) : (half + 1) * (HALF // 16)])
+            for half in range(2)
+        ]
+        for stage in range(3):
+            for half in range(2):
+                total = psum.tile([P, HALF], F32, name=f"total{stage}_{half}")
+                nc.tensor.matmul(total[:], weights[stage][:], moving[half])
+                if stage < 2:
+                    hidden = held.tile([P, HALF], BF16, name=f"hidden{stage}_{half}")
+                    biased = hidden[:]
+                else:
+                    biased = result[:, half * HALF : (half + 1) * HALF]
+                if half == 0:
+                    nc.vector.tensor_scalar(biased, total[:], biases[stage][:], None, ADD)
+                else:
+                    nc.scalar.activation(biased, total[:], IDENTITY, bias=biases[stage][:])
+                moving[half] = biased
         nc.sync.dma_start(out, result[:])

@@ -11,7 +11,6 @@ BF16 = mybir.dt.bfloat16
 F32 = mybir.dt.float32
 U16 = mybir.dt.uint16
 ADD = mybir.AluOpType.add
-IDENTITY = mybir.ActivationFunctionType.Identity
 
 
 def tile_switchnet_fstar_kernel(tc, table, k1, b1, k2, b2, k3, b3, offs, out):
@@ -27,7 +26,7 @@ def tile_switchnet_fstar_kernel(tc, table, k1, b1, k2, b2, k3, b3, offs, out):
         weights = []
         biases = []
         for stage, (k, b, queue) in enumerate(
-            ((k1, b1, nc.scalar), (k2, b2, nc.scalar), (k3, b3, nc.gpsimd))
+            ((k1, b1, nc.scalar), (k2, b2, nc.scalar), (k3, b3, nc.sync))
         ):
             weight = held.tile([P, P], BF16, name=f"weight{stage}")
             queue.dma_start(weight[:], k)
@@ -51,9 +50,6 @@ def tile_switchnet_fstar_kernel(tc, table, k1, b1, k2, b2, k3, b3, offs, out):
                     biased = hidden[:]
                 else:
                     biased = result[:, half * HALF : (half + 1) * HALF]
-                if half == 0:
-                    nc.vector.tensor_scalar(biased, total[:], biases[stage][:], None, ADD)
-                else:
-                    nc.scalar.activation(biased, total[:], IDENTITY, bias=biases[stage][:])
+                nc.vector.tensor_scalar(biased, total[:], biases[stage][:], None, ADD)
                 moving[half] = biased
         nc.sync.dma_start(out, result[:])

@@ -52,4 +52,6 @@ def tile_switchnet_fstar_kernel(tc, table, k1, b1, k2, b2, k3, b3, offs, out):
                     biased = result[:, half * HALF : (half + 1) * HALF]
                 nc.vector.tensor_scalar(biased, total[:], biases[stage][:], None, ADD)
                 moving[half] = biased
-        nc.sync.dma_start(out, result[:])
+        for half, queue in enumerate((nc.sync, nc.scalar)):
+            columns = slice(half * HALF, (half + 1) * HALF)
+            queue.dma_start(out[:, columns], result[:, columns])

@@ -3,7 +3,8 @@ import concourse.mybir as mybir
 P = 128
 S = 1024
 N = 256
-HALF = N // 2
+PIECES = 4
+WIDTH = N // PIECES
 
 FLOPS = 3 * 2 * P * P * N
 
@@ -17,7 +18,7 @@ def tile_switchnet_fstar_kernel(tc, table, k1, b1, k2, b2, k3, b3, offs, out):
     nc = tc.nc
     with (
         tc.tile_pool(name="held", bufs=1) as held,
-        tc.psum_pool(name="psum", bufs=1) as psum,
+        tc.psum_pool(name="psum", bufs=8) as psum,
     ):
         offsets = held.tile([P, N // 16], U16, name="offsets")
         nc.sync.dma_start(offsets[:], offs)
@@ -38,20 +39,18 @@ def tile_switchnet_fstar_kernel(tc, table, k1, b1, k2, b2, k3, b3, offs, out):
         result = held.tile([P, N], F32, name="result")
 
         moving = [
-            samples[:].indirect(offsets[:, half * (HALF // 16) : (half + 1) * (HALF // 16)])
-            for half in range(2)
+            samples[:].indirect(offsets[:, piece * (WIDTH // 16) : (piece + 1) * (WIDTH // 16)])
+            for piece in range(PIECES)
         ]
         for stage in range(3):
-            for half in range(2):
-                total = psum.tile([P, HALF], F32, name=f"total{stage}_{half}")
-                nc.tensor.matmul(total[:], weights[stage][:], moving[half])
+            for piece in range(PIECES):
+                total = psum.tile([P, WIDTH], F32, name="total")
+                nc.tensor.matmul(total[:], weights[stage][:], moving[piece])
                 if stage < 2:
-                    hidden = held.tile([P, HALF], BF16, name=f"hidden{stage}_{half}")
+                    hidden = held.tile([P, WIDTH], BF16, name=f"hidden{stage}_{piece}")
                     biased = hidden[:]
                 else:
-                    biased = result[:, half * HALF : (half + 1) * HALF]
+                    biased = result[:, piece * WIDTH : (piece + 1) * WIDTH]
                 nc.vector.tensor_scalar(biased, total[:], biases[stage][:], None, ADD)
-                moving[half] = biased
-        for half, queue in enumerate((nc.sync, nc.scalar)):
-            columns = slice(half * HALF, (half + 1) * HALF)
-            queue.dma_start(out[:, columns], result[:, columns])
+                moving[piece] = biased
+        nc.sync.dma_start(out, result[:])

@@ -3,8 +3,8 @@ import concourse.mybir as mybir
 P = 128
 S = 1024
 N = 256
-PIECES = 4
-WIDTH = N // PIECES
+HALF = N // 2
+WARM_MATMULS = 16
 
 FLOPS = 3 * 2 * P * P * N
 
@@ -18,7 +18,7 @@ def tile_switchnet_fstar_kernel(tc, table, k1, b1, k2, b2, k3, b3, offs, out):
     nc = tc.nc
     with (
         tc.tile_pool(name="held", bufs=1) as held,
-        tc.psum_pool(name="psum", bufs=8) as psum,
+        tc.psum_pool(name="psum", bufs=1) as psum,
     ):
         offsets = held.tile([P, N // 16], U16, name="offsets")
         nc.sync.dma_start(offsets[:], offs)
@@ -36,21 +36,27 @@ def tile_switchnet_fstar_kernel(tc, table, k1, b1, k2, b2, k3, b3, offs, out):
             weights.append(weight)
             biases.append(bias)
 
+        zeros = held.tile([P, P], BF16, name="zeros")
+        nc.vector.memset(zeros[:], 0.0)
+        unread = psum.tile([P, P], F32, name="unread")
+        for turn in range(WARM_MATMULS):
+            nc.tensor.matmul(unread[:], zeros[:], zeros[:])
+
         result = held.tile([P, N], F32, name="result")
 
         moving = [
-            samples[:].indirect(offsets[:, piece * (WIDTH // 16) : (piece + 1) * (WIDTH // 16)])
-            for piece in range(PIECES)
+            samples[:].indirect(offsets[:, half * (HALF // 16) : (half + 1) * (HALF // 16)])
+            for half in range(2)
         ]
         for stage in range(3):
-            for piece in range(PIECES):
-                total = psum.tile([P, WIDTH], F32, name="total")
-                nc.tensor.matmul(total[:], weights[stage][:], moving[piece])
+            for half in range(2):
+                total = psum.tile([P, HALF], F32, name=f"total{stage}_{half}")
+                nc.tensor.matmul(total[:], weights[stage][:], moving[half])
                 if stage < 2:
-                    hidden = held.tile([P, WIDTH], BF16, name=f"hidden{stage}_{piece}")
+                    hidden = held.tile([P, HALF], BF16, name=f"hidden{stage}_{half}")
                     biased = hidden[:]
                 else:
-                    biased = result[:, piece * WIDTH : (piece + 1) * WIDTH]
+                    biased = result[:, half * HALF : (half + 1) * HALF]
                 nc.vector.tensor_scalar(biased, total[:], biases[stage][:], None, ADD)
-                moving[piece] = biased
+                moving[half] = biased
         nc.sync.dma_start(out, result[:])

@@ -3,7 +3,8 @@ import concourse.mybir as mybir
 P = 128
 S = 1024
 N = 256
-HALF = N // 2
+PIECES = 4
+WIDTH = N // PIECES
 WARM_MATMULS = 16
 
 FLOPS = 3 * 2 * P * P * N
@@ -12,6 +13,7 @@ BF16 = mybir.dt.bfloat16
 F32 = mybir.dt.float32
 U16 = mybir.dt.uint16
 ADD = mybir.AluOpType.add
+IDENTITY = mybir.ActivationFunctionType.Identity
 
 
 def tile_switchnet_fstar_kernel(tc, table, k1, b1, k2, b2, k3, b3, offs, out):
@@ -27,7 +29,7 @@ def tile_switchnet_fstar_kernel(tc, table, k1, b1, k2, b2, k3, b3, offs, out):
         weights = []
         biases = []
         for stage, (k, b, queue) in enumerate(
-            ((k1, b1, nc.scalar), (k2, b2, nc.scalar), (k3, b3, nc.sync))
+            ((k1, b1, nc.scalar), (k2, b2, nc.sync), (k3, b3, nc.sync))
         ):
             weight = held.tile([P, P], BF16, name=f"weight{stage}")
             queue.dma_start(weight[:], k)
@@ -36,27 +38,33 @@ def tile_switchnet_fstar_kernel(tc, table, k1, b1, k2, b2, k3, b3, offs, out):
             weights.append(weight)
             biases.append(bias)
 
-        zeros = held.tile([P, P], BF16, name="zeros")
+        zeros = held.tile([P, 128], BF16, name="zeros")
         nc.vector.memset(zeros[:], 0.0)
-        unread = psum.tile([P, P], F32, name="unread")
+        unread = psum.tile([P, 128], F32, name="unread")
         for turn in range(WARM_MATMULS):
-            nc.tensor.matmul(unread[:], zeros[:], zeros[:])
+            nc.tensor.matmul(unread[:], zeros[:, 0:P], zeros[:])
+
+        primed = held.tile([P, 1], BF16, name="primed")
+        nc.scalar.activation(primed[:], zeros[:, 0:1], IDENTITY)
 
         result = held.tile([P, N], F32, name="result")
 
         moving = [
-            samples[:].indirect(offsets[:, half * (HALF // 16) : (half + 1) * (HALF // 16)])
-            for half in range(2)
+            samples[:].indirect(offsets[:, piece * (WIDTH // 16) : (piece + 1) * (WIDTH // 16)])
+            for piece in range(PIECES)
         ]
+        totals = [psum.tile([P, WIDTH], F32, name=f"total{piece}") for piece in range(PIECES)]
         for stage in range(3):
-            for half in range(2):
-                total = psum.tile([P, HALF], F32, name=f"total{stage}_{half}")
-                nc.tensor.matmul(total[:], weights[stage][:], moving[half])
+            for piece in range(PIECES):
+                nc.tensor.matmul(totals[piece][:], weights[stage][:], moving[piece])
                 if stage < 2:
-                    hidden = held.tile([P, HALF], BF16, name=f"hidden{stage}_{half}")
+                    hidden = held.tile([P, WIDTH], BF16, name=f"hidden{stage}_{piece}")
                     biased = hidden[:]
                 else:
-                    biased = result[:, half * HALF : (half + 1) * HALF]
-                nc.vector.tensor_scalar(biased, total[:], biases[stage][:], None, ADD)
-                moving[half] = biased
+                    biased = result[:, piece * WIDTH : (piece + 1) * WIDTH]
+                if piece % 2 == 0:
+                    nc.vector.tensor_scalar(biased, totals[piece][:], biases[stage][:], None, ADD)
+                else:
+                    nc.scalar.activation(biased, totals[piece][:], IDENTITY, bias=biases[stage][:])
+                moving[piece] = biased
         nc.sync.dma_start(out, result[:])

@@ -67,4 +67,5 @@ def tile_switchnet_fstar_kernel(tc, table, k1, b1, k2, b2, k3, b3, offs, out):
                 else:
                     nc.scalar.activation(biased, totals[piece][:], IDENTITY, bias=biases[stage][:])
                 moving[piece] = biased
-        nc.sync.dma_start(out, result[:])
+                if stage == 2:
+                    nc.sync.dma_start(out[:, piece * WIDTH : (piece + 1) * WIDTH], biased)

@@ -25,7 +25,8 @@ def tile_switchnet_fstar_kernel(tc, table, k1, b1, k2, b2, k3, b3, offs, out):
         offsets = held.tile([P, N // 16], U16, name="offsets")
         nc.sync.dma_start(offsets[:], offs)
         samples = held.tile([P, S], BF16, name="samples")
-        nc.sync.dma_start(samples[:], table)
+        nc.sync.dma_start(samples[:, 0 : S // 2], table[:, 0 : S // 2])
+        nc.scalar.dma_start(samples[:, S // 2 : S], table[:, S // 2 : S])
         weights = []
         biases = []
         for stage, (k, b, queue) in enumerate(

@@ -13,7 +13,6 @@ BF16 = mybir.dt.bfloat16
 F32 = mybir.dt.float32
 U16 = mybir.dt.uint16
 ADD = mybir.AluOpType.add
-IDENTITY = mybir.ActivationFunctionType.Identity
 
 
 def tile_switchnet_fstar_kernel(tc, table, k1, b1, k2, b2, k3, b3, offs, out):
@@ -22,11 +21,11 @@ def tile_switchnet_fstar_kernel(tc, table, k1, b1, k2, b2, k3, b3, offs, out):
         tc.tile_pool(name="held", bufs=1) as held,
         tc.psum_pool(name="psum", bufs=1) as psum,
     ):
-        offsets = held.tile([P, N // 16], U16, name="offsets")
-        nc.sync.dma_start(offsets[:], offs)
         samples = held.tile([P, S], BF16, name="samples")
         nc.sync.dma_start(samples[:, 0 : S // 2], table[:, 0 : S // 2])
         nc.scalar.dma_start(samples[:, S // 2 : S], table[:, S // 2 : S])
+        offsets = held.tile([P, N // 16], U16, name="offsets")
+        nc.sync.dma_start(offsets[:], offs)
         weights = []
         biases = []
         for stage, (k, b, queue) in enumerate(
@@ -45,8 +44,6 @@ def tile_switchnet_fstar_kernel(tc, table, k1, b1, k2, b2, k3, b3, offs, out):
         for turn in range(WARM_MATMULS):
             nc.tensor.matmul(unread[:], zeros[:, 0:P], zeros[:])
 
-        primed = held.tile([P, 1], BF16, name="primed")
-        nc.scalar.activation(primed[:], zeros[:, 0:1], IDENTITY)
 
         result = held.tile([P, N], F32, name="result")
 
@@ -63,10 +60,7 @@ def tile_switchnet_fstar_kernel(tc, table, k1, b1, k2, b2, k3, b3, offs, out):
                     biased = hidden[:]
                 else:
                     biased = result[:, piece * WIDTH : (piece + 1) * WIDTH]
-                if piece % 2 == 0:
-                    nc.vector.tensor_scalar(biased, totals[piece][:], biases[stage][:], None, ADD)
-                else:
-                    nc.scalar.activation(biased, totals[piece][:], IDENTITY, bias=biases[stage][:])
+                nc.vector.tensor_scalar(biased, totals[piece][:], biases[stage][:], None, ADD)
                 moving[piece] = biased
                 if stage == 2:
                     nc.sync.dma_start(out[:, piece * WIDTH : (piece + 1) * WIDTH], biased)

@@ -22,19 +22,22 @@ def tile_switchnet_fstar_kernel(tc, table, k1, b1, k2, b2, k3, b3, offs, out):
         tc.psum_pool(name="psum", bufs=1) as psum,
     ):
         samples = held.tile([P, S], BF16, name="samples")
-        nc.sync.dma_start(samples[:, 0 : S // 2], table[:, 0 : S // 2])
-        nc.scalar.dma_start(samples[:, S // 2 : S], table[:, S // 2 : S])
+        nc.sync.dma_start(samples[:], table)
         offsets = held.tile([P, N // 16], U16, name="offsets")
         nc.sync.dma_start(offsets[:], offs)
         weights = []
         biases = []
-        for stage, (k, b, queue) in enumerate(
-            ((k1, b1, nc.scalar), (k2, b2, nc.sync), (k3, b3, nc.sync))
+        for stage, (k, k_queue, b, b_queue) in enumerate(
+            (
+                (k1, nc.scalar, b1, nc.scalar),
+                (k2, nc.sync, b2, nc.sync),
+                (k3, nc.sync, b3, nc.sync),
+            )
         ):
             weight = held.tile([P, P], BF16, name=f"weight{stage}")
-            queue.dma_start(weight[:], k)
+            k_queue.dma_start(weight[:], k)
             bias = held.tile([P, 1], F32, name=f"bias{stage}")
-            queue.dma_start(bias[:], b)
+            b_queue.dma_start(bias[:], b)
             weights.append(weight)
             biases.append(bias)
 

@@ -66,4 +66,6 @@ def tile_switchnet_fstar_kernel(tc, table, k1, b1, k2, b2, k3, b3, offs, out):
                 nc.vector.tensor_scalar(biased, totals[piece][:], biases[stage][:], None, ADD)
                 moving[piece] = biased
                 if stage == 2:
-                    nc.sync.dma_start(out[:, piece * WIDTH : (piece + 1) * WIDTH], biased)
+                    if piece % 2 == 1:
+                        pair = slice((piece - 1) * WIDTH, (piece + 1) * WIDTH)
+                        nc.sync.dma_start(out[:, pair], result[:, pair])

@@ -3,8 +3,8 @@ import concourse.mybir as mybir
 P = 128
 S = 1024
 N = 256
-PIECES = 4
-WIDTH = N // PIECES
+WIDTHS = (64, 32, 32)
+BANKS = 8
 WARM_MATMULS = 16
 
 FLOPS = 3 * 2 * P * P * N
@@ -41,31 +41,30 @@ def tile_switchnet_fstar_kernel(tc, table, k1, b1, k2, b2, k3, b3, offs, out):
             weights.append(weight)
             biases.append(bias)
 
+        totals = [psum.tile([P, 128], F32, name=f"total{bank}") for bank in range(BANKS)]
+
         zeros = held.tile([P, 128], BF16, name="zeros")
         nc.vector.memset(zeros[:], 0.0)
-        unread = psum.tile([P, 128], F32, name="unread")
         for turn in range(WARM_MATMULS):
-            nc.tensor.matmul(unread[:], zeros[:, 0:P], zeros[:])
+            nc.tensor.matmul(totals[-1][:], zeros[:, 0:P], zeros[:])
 
 
         result = held.tile([P, N], F32, name="result")
+        hidden = [held.tile([P, N], BF16, name=f"hidden{stage}") for stage in range(2)]
 
-        moving = [
-            samples[:].indirect(offsets[:, piece * (WIDTH // 16) : (piece + 1) * (WIDTH // 16)])
-            for piece in range(PIECES)
-        ]
-        totals = [psum.tile([P, WIDTH], F32, name=f"total{piece}") for piece in range(PIECES)]
         for stage in range(3):
-            for piece in range(PIECES):
-                nc.tensor.matmul(totals[piece][:], weights[stage][:], moving[piece])
-                if stage < 2:
-                    hidden = held.tile([P, WIDTH], BF16, name=f"hidden{stage}_{piece}")
-                    biased = hidden[:]
+            width = WIDTHS[stage]
+            for first in range(0, N, width):
+                columns = slice(first, first + width)
+                if stage == 0:
+                    moving = samples[:].indirect(offsets[:, first // 16 : (first + width) // 16])
                 else:
-                    biased = result[:, piece * WIDTH : (piece + 1) * WIDTH]
-                nc.vector.tensor_scalar(biased, totals[piece][:], biases[stage][:], None, ADD)
-                moving[piece] = biased
-                if stage == 2:
-                    if piece % 2 == 1:
-                        pair = slice((piece - 1) * WIDTH, (piece + 1) * WIDTH)
-                        nc.sync.dma_start(out[:, pair], result[:, pair])
+                    moving = hidden[stage - 1][:, columns]
+                total = totals[first * BANKS // N][:, 0:width]
+                nc.tensor.matmul(total, weights[stage][:], moving)
+                biased = result[:, columns] if stage == 2 else hidden[stage][:, columns]
+                nc.vector.tensor_scalar(biased, total, biases[stage][:], None, ADD)
+                end = first + width
+                if stage == 2 and end % (N // 2) == 0:
+                    half = slice(end - N // 2, end)
+                    nc.sync.dma_start(out[:, half], result[:, half])

@@ -3,7 +3,12 @@ import concourse.mybir as mybir
 P = 128
 S = 1024
 N = 256
-WIDTHS = (64, 32, 32)
+CUTS = (
+    (0, 128, N),
+    range(0, N + 1, 32),
+    range(0, N + 1, 32),
+)
+ADDED = (32, 32, 32)
 BANKS = 8
 WARM_MATMULS = 16
 
@@ -41,30 +46,36 @@ def tile_switchnet_fstar_kernel(tc, table, k1, b1, k2, b2, k3, b3, offs, out):
             weights.append(weight)
             biases.append(bias)
 
-        totals = [psum.tile([P, 128], F32, name=f"total{bank}") for bank in range(BANKS)]
+        totals = [psum.tile([P, 256], F32, name=f"total{bank}") for bank in range(BANKS)]
 
         zeros = held.tile([P, 128], BF16, name="zeros")
         nc.vector.memset(zeros[:], 0.0)
         for turn in range(WARM_MATMULS):
-            nc.tensor.matmul(totals[-1][:], zeros[:, 0:P], zeros[:])
+            nc.tensor.matmul(totals[-1][:, 0:P], zeros[:, 0:P], zeros[:])
 
 
         result = held.tile([P, N], F32, name="result")
         hidden = [held.tile([P, N], BF16, name=f"hidden{stage}") for stage in range(2)]
 
         for stage in range(3):
-            width = WIDTHS[stage]
-            for first in range(0, N, width):
-                columns = slice(first, first + width)
+            pieces = list(zip(CUTS[stage][:-1], CUTS[stage][1:]))
+            for piece, (first, last) in enumerate(pieces):
                 if stage == 0:
-                    moving = samples[:].indirect(offsets[:, first // 16 : (first + width) // 16])
+                    moving = samples[:].indirect(offsets[:, first // 16 : last // 16])
                 else:
-                    moving = hidden[stage - 1][:, columns]
-                total = totals[first * BANKS // N][:, 0:width]
-                nc.tensor.matmul(total, weights[stage][:], moving)
-                biased = result[:, columns] if stage == 2 else hidden[stage][:, columns]
-                nc.vector.tensor_scalar(biased, total, biases[stage][:], None, ADD)
-                end = first + width
-                if stage == 2 and end % (N // 2) == 0:
-                    half = slice(end - N // 2, end)
+                    moving = hidden[stage - 1][:, first:last]
+                total = totals[BANKS - len(pieces) + piece]
+                nc.tensor.matmul(total[:, 0 : last - first], weights[stage][:], moving)
+                biased = result if stage == 2 else hidden[stage]
+                for start in range(first, last, ADDED[stage]):
+                    end = min(start + ADDED[stage], last)
+                    nc.vector.tensor_scalar(
+                        biased[:, start:end],
+                        total[:, start - first : end - first],
+                        biases[stage][:],
+                        None,
+                        ADD,
+                    )
+                if stage == 2 and last % (N // 2) == 0:
+                    half = slice(last - N // 2, last)
                     nc.sync.dma_start(out[:, half], result[:, half])

@@ -10,7 +10,7 @@ CUTS = (
 )
 ADDED = (32, 32, 32)
 BANKS = 8
-WARM_MATMULS = 16
+WARM_MATMULS = 4
 
 FLOPS = 3 * 2 * P * P * N
 
@@ -46,12 +46,12 @@ def tile_switchnet_fstar_kernel(tc, table, k1, b1, k2, b2, k3, b3, offs, out):
             weights.append(weight)
             biases.append(bias)
 
-        totals = [psum.tile([P, 256], F32, name=f"total{bank}") for bank in range(BANKS)]
+        totals = [psum.tile([P, 512], F32, name=f"total{bank}") for bank in range(BANKS)]
 
-        zeros = held.tile([P, 128], BF16, name="zeros")
+        zeros = held.tile([P, P], BF16, name="zeros")
         nc.vector.memset(zeros[:], 0.0)
         for turn in range(WARM_MATMULS):
-            nc.tensor.matmul(totals[-1][:, 0:P], zeros[:, 0:P], zeros[:])
+            nc.tensor.matmul(totals[-1][:], zeros[:], zeros[:, 0:1].to_broadcast([P, 512]))
 
 
         result = held.tile([P, N], F32, name="result")

import concourse.mybir as mybir

P = 128
S = 1024
N = 256
CUTS = (
    (0, 128, N),
    range(0, N + 1, 32),
    range(0, N + 1, 32),
)
ADDED = (32, 32, 32)
BANKS = 8
WARM_MATMULS = 4

FLOPS = 3 * 2 * P * P * N

BF16 = mybir.dt.bfloat16
F32 = mybir.dt.float32
U16 = mybir.dt.uint16
ADD = mybir.AluOpType.add


def tile_switchnet_fstar_kernel(tc, table, k1, b1, k2, b2, k3, b3, offs, out):
    nc = tc.nc
    with (
        tc.tile_pool(name="held", bufs=1) as held,
        tc.psum_pool(name="psum", bufs=1) as psum,
    ):
        samples = held.tile([P, S], BF16, name="samples")
        nc.sync.dma_start(samples[:], table)
        offsets = held.tile([P, N // 16], U16, name="offsets")
        nc.sync.dma_start(offsets[:], offs)
        weights = []
        biases = []
        for stage, (k, k_queue, b, b_queue) in enumerate(
            (
                (k1, nc.scalar, b1, nc.scalar),
                (k2, nc.sync, b2, nc.sync),
                (k3, nc.sync, b3, nc.sync),
            )
        ):
            weight = held.tile([P, P], BF16, name=f"weight{stage}")
            k_queue.dma_start(weight[:], k)
            bias = held.tile([P, 1], F32, name=f"bias{stage}")
            b_queue.dma_start(bias[:], b)
            weights.append(weight)
            biases.append(bias)

        totals = [psum.tile([P, 512], F32, name=f"total{bank}") for bank in range(BANKS)]

        zeros = held.tile([P, P], BF16, name="zeros")
        nc.vector.memset(zeros[:], 0.0)
        for turn in range(WARM_MATMULS):
            nc.tensor.matmul(totals[-1][:], zeros[:], zeros[:, 0:1].to_broadcast([P, 512]))


        result = held.tile([P, N], F32, name="result")
        hidden = [held.tile([P, N], BF16, name=f"hidden{stage}") for stage in range(2)]

        for stage in range(3):
            pieces = list(zip(CUTS[stage][:-1], CUTS[stage][1:]))
            for piece, (first, last) in enumerate(pieces):
                if stage == 0:
                    moving = samples[:].indirect(offsets[:, first // 16 : last // 16])
                else:
                    moving = hidden[stage - 1][:, first:last]
                total = totals[BANKS - len(pieces) + piece]
                nc.tensor.matmul(total[:, 0 : last - first], weights[stage][:], moving)
                biased = result if stage == 2 else hidden[stage]
                for start in range(first, last, ADDED[stage]):
                    end = min(start + ADDED[stage], last)
                    nc.vector.tensor_scalar(
                        biased[:, start:end],
                        total[:, start - first : end - first],
                        biases[stage][:],
                        None,
                        ADD,
                    )
                if stage == 2 and last % (N // 2) == 0:
                    half = slice(last - N // 2, last)
                    nc.sync.dma_start(out[:, half], result[:, half])
